import numpy as np
import ml_dtypes


def mxq(x, axis, fmt="e4m3"):
    dtype, down = {"e4m3": (ml_dtypes.float8_e4m3fn, 7), "e5m2": (ml_dtypes.float8_e5m2, 14)}[fmt]
    v = np.moveaxis(np.asarray(x, np.float32).astype(ml_dtypes.bfloat16).astype(np.float64), axis, -1)
    blocks = v.reshape(v.shape[:-1] + (-1, 32))
    amax = np.abs(blocks).max(-1, keepdims=True)
    byte = np.maximum(np.where(amax > 0, np.frexp(amax)[1] - 1 + 127, 0) - down, 1)
    scale = np.exp2(byte - 127.0)
    codes = (blocks / scale).astype(np.float32).astype(dtype).astype(np.float64)
    return np.moveaxis((codes * scale).reshape(v.shape), -1, axis)


WIDE = False


def mx_kscale(k):
    if not WIDE:
        return np.ones(k)
    levels = np.array([10, -10, 5, -5, 0])
    a = np.random.permutation(np.resize(levels, k // 512 * 4)).reshape(k // 512, 4)
    idx = np.arange(k)
    return np.exp2(a[idx // 512, idx % 128 // 32])


BF16 = ml_dtypes.bfloat16


def bf(x):
    return np.asarray(x, np.float32).astype(BF16)


def f64(x):
    return np.asarray(x).astype(np.float64)


E2M1 = np.array([0.0, 0.5, 1.0, 1.5, 2.0, 3.0, 4.0, 6.0, -0.0, -0.5, -1.0, -1.5, -2.0, -3.0, -4.0, -6.0])


def pack_weight(w, fmt):
    k, n = w.shape
    w = f64(bf(w)).reshape(k // 32, 32, n)
    amax = np.abs(w).max(1)
    if fmt == "e4m3":
        byte = np.frexp(amax)[1] - 1 + 127 - 7
    else:
        mant, ex = np.frexp(amax / 6.0)
        byte = np.where(mant > 0.5, ex, ex - 1) + 127
    byte = np.clip(np.where(amax > 0, byte, 1), 1, 254)
    scaled = (w * np.exp2(127.0 - byte)[:, None, :]).reshape(k, n).astype(np.float32)
    by_word = np.ascontiguousarray(scaled.reshape(k // 512, 128, 4, n).transpose(0, 1, 3, 2))
    if fmt == "e4m3":
        words = by_word.astype(ml_dtypes.float8_e4m3fn).view(np.uint8)
    else:
        c = by_word.astype(ml_dtypes.float4_e2m1fn).view(np.uint8) & 0xF
        words = c[..., 0::2] | (c[..., 1::2] << 4)
    return np.ascontiguousarray(words), np.ascontiguousarray(byte.astype(np.uint8).reshape(k // 512, 16, n))


def unpack_weight(words, scales, fmt):
    g, p, n, _ = words.shape
    if fmt == "e4m3":
        vals = np.ascontiguousarray(words).view(ml_dtypes.float8_e4m3fn).astype(np.float64)
    else:
        nib = np.empty((g, p, n, 4), np.uint8)
        nib[..., 0::2] = words & 0xF
        nib[..., 1::2] = words >> 4
        vals = E2M1[nib]
    vals = vals * np.repeat(np.exp2(scales.astype(np.float64) - 127.0), 8, axis=1)[..., None]
    return vals.transpose(0, 1, 3, 2).reshape(g * 512, n)

def pack4(w):
    words, scales = pack_weight(w, "e2m1")
    return words.reshape(words.shape[0], 128, -1), scales


def unpack4(words, scales):
    return unpack_weight(words.reshape(words.shape[0], 128, -1, 2), scales, "e2m1")


B, O, A, H, Z = 256, 512, 512, 1536, 512
I = O + Z + A


def sigmoid(v):
    return 1.0 / (1.0 + np.exp(-v))


def setup_inputs():
    s = mx_kscale(I)
    x_t = bf(np.random.standard_normal((B, O)) * s[:O])
    z_t = bf(np.random.standard_normal((B, Z)) * 1.4 * s[O:O + Z])
    a_prev = bf(np.random.standard_normal((B, A)) * s[O + Z:])
    h_prev = bf(np.random.standard_normal((B, H)))
    w_ih = np.random.standard_normal((3 * H, I)) / np.sqrt(I) / s[None, :]
    w_hh = np.random.standard_normal((3 * H, H)) / np.sqrt(H)
    b_ih = bf(np.random.standard_normal(3 * H) * 0.2)
    b_hh = bf(np.random.standard_normal(3 * H) * 0.2)
    w_ih_words, w_ih_scales = pack4(np.ascontiguousarray(w_ih.T))
    w_hh_words, w_hh_scales = pack4(np.ascontiguousarray(w_hh.T))
    return {
        "x_t": x_t,
        "z_t": z_t,
        "a_prev": a_prev,
        "h_prev": h_prev,
        "w_ih_words": w_ih_words,
        "w_ih_scales": w_ih_scales,
        "w_hh_words": w_hh_words,
        "w_hh_scales": w_hh_scales,
        "b_ih": b_ih,
        "b_hh": b_hh,
    }


def reference(x_t, z_t, a_prev, h_prev, w_ih_words, w_ih_scales, w_hh_words, w_hh_scales, b_ih, b_hh):
    h = f64(h_prev)
    rnn_in = np.concatenate([f64(x_t), f64(z_t), f64(a_prev)], -1)
    gi = (mxq(rnn_in, 1, "e4m3") @ unpack4(w_ih_words, w_ih_scales)) + f64(b_ih)
    gh = (mxq(h, 1, "e4m3") @ unpack4(w_hh_words, w_hh_scales)) + f64(b_hh)
    i_r, i_z, i_n = gi[:, :H], gi[:, H:2 * H], gi[:, 2 * H:]
    h_r, h_z, h_n = gh[:, :H], gh[:, H:2 * H], gh[:, 2 * H:]
    r = sigmoid(i_r + h_r)
    zg = sigmoid(i_z + h_z)
    n = np.tanh(i_n + r * h_n)
    return (1.0 - zg) * n + zg * h

@@ -1,0 +1,250 @@
+from contextlib import ExitStack
+
+import concourse.mybir as mybir
+from concourse.masks import make_identity
+
+F32 = mybir.dt.float32
+BF16 = mybir.dt.bfloat16
+I32 = mybir.dt.int32
+U32 = mybir.dt.uint32
+U8 = mybir.dt.uint8
+FP8X4 = mybir.dt.float8_e4m3fn_x4
+FP4X4 = mybir.dt.float4_e2m1fn_x4
+ALU = mybir.AluOpType
+ACT = mybir.ActivationFunctionType
+
+P = 128
+BATCH_TILES = 2
+HIDDEN = 1536
+K_PASS = 512
+PASSES = 3
+N_TILE = 512
+CHUNKS = HIDDEN // N_TILE
+GATE_R, GATE_Z, GATE_N = 0, 1, 2
+BIAS_ROWS = 3 * CHUNKS
+
+FLOPS = 2 * 2 * 256 * 1536 * 4608
+
+
+def tile_vrnncell_pc_kernel(
+    tc, x_t, z_t, a_prev, h_prev, w_ih_words, w_ih_scales, w_hh_words, w_hh_scales, b_ih, b_hh, out
+):
+    nc = tc.nc
+    with ExitStack() as ctx:
+        keep = ctx.enter_context(tc.tile_pool(name="keep", bufs=1))
+        stage = ctx.enter_context(tc.tile_pool(name="stage", bufs=3))
+        work = ctx.enter_context(tc.tile_pool(name="work", bufs=4))
+        banks = ctx.enter_context(tc.psum_pool(name="banks", bufs=8))
+        ctx.enter_context(tc.manual_schedule())
+
+        bias_rows = keep.tile([P, N_TILE], BF16, name="bias_rows")
+        nc.vector.memset(bias_rows[:].bitcast(I32), 0)
+        nc.scalar.dma_start(out=bias_rows[0:BIAS_ROWS, :], in_=b_ih.rearrange("(s n) -> s n", n=N_TILE))
+        nc.scalar.dma_start(
+            out=bias_rows[BIAS_ROWS : 2 * BIAS_ROWS, :], in_=b_hh.rearrange("(s n) -> s n", n=N_TILE)
+        )
+        warm = keep.tile([P, 1], F32, name="warm")
+        nc.vector.memset(warm[:], 0.0)
+        nc.scalar.activation(out=warm[:], in_=warm[:], func=ACT.Sigmoid)
+        ident_bf16 = keep.tile([P, P], BF16, name="ident_bf16")
+        make_identity(nc, ident_bf16[:])
+        ident_f32 = keep.tile([P, P], F32, name="ident_f32")
+        make_identity(nc, ident_f32[:])
+
+        def load_activation(dram, features, name):
+            sb = keep.tile([P, BATCH_TILES, features], BF16, name=name)
+            nc.sync.dma_start(out=sb[:], in_=dram.rearrange("(t p) k -> p t k", p=P))
+            return sb
+
+        x_sb = load_activation(x_t, K_PASS, "x_sb")
+        z_sb = load_activation(z_t, K_PASS, "z_sb")
+        a_sb = load_activation(a_prev, K_PASS, "a_sb")
+        h_sb = load_activation(h_prev, HIDDEN, "h_sb")
+
+        def load_scales(scales, gate, name):
+            plane = keep.tile([P, PASSES, HIDDEN], U8, name=name, align_bytes=64)
+            nc.vector.memset(plane[:].bitcast(I32), 0)
+            columns = scales[:, :, HIDDEN * gate : HIDDEN * (gate + 1)]
+            for q in range(8):
+                partition = 32 * (q // 4) + q % 4
+                nc.sync.dma_start(
+                    out=plane[partition:P:64, :, :].bitcast(I32),
+                    in_=columns[:, q:16:8, :].rearrange("g j n -> j g n").bitcast(I32),
+                )
+            return plane
+
+        def load_words(words, gate, name):
+            tiles = []
+            for g in range(PASSES):
+                w = keep.tile([P, 2 * HIDDEN], U8, name="%s_%d" % (name, g), align_bytes=64)
+                nc.sync.dma_start(
+                    out=w[:].bitcast(I32),
+                    in_=words[g, :, 2 * HIDDEN * gate : 2 * HIDDEN * (gate + 1)].bitcast(I32),
+                )
+                tiles.append(w)
+            return tiles
+
+        ih_plane, hh_plane, ih_words, hh_words = {}, {}, {}, {}
+        ih_plane[GATE_N] = load_scales(w_ih_scales, GATE_N, "ih_plane_n")
+        ih_words[GATE_N] = load_words(w_ih_words, GATE_N, "ih_words_n")
+        hh_plane[GATE_N] = load_scales(w_hh_scales, GATE_N, "hh_plane_n")
+        hh_words[GATE_N] = load_words(w_hh_words, GATE_N, "hh_words_n")
+        for gate, label in ((GATE_R, "r"), (GATE_Z, "z")):
+            ih_plane[gate] = load_scales(w_ih_scales, gate, "ih_plane_" + label)
+            hh_plane[gate] = load_scales(w_hh_scales, gate, "hh_plane_" + label)
+            ih_words[gate] = load_words(w_ih_words, gate, "ih_words_" + label)
+            hh_words[gate] = load_words(w_hh_words, gate, "hh_words_" + label)
+
+        both = keep.tile([P, 2 * CHUNKS], BF16, name="both")
+        nc.vector.tensor_tensor(
+            out=both[:],
+            in0=ident_bf16[:, 0 : 2 * CHUNKS],
+            in1=ident_bf16[:, BIAS_ROWS : BIAS_ROWS + 2 * CHUNKS],
+            op=ALU.add,
+        )
+
+        def selector(kind, chunk):
+            if kind == "i_n":
+                row = CHUNKS * GATE_N + chunk
+                return ident_bf16[:, row : row + 1]
+            if kind == "h_n":
+                row = BIAS_ROWS + CHUNKS * GATE_N + chunk
+                return ident_bf16[:, row : row + 1]
+            row = CHUNKS * (GATE_R if kind == "r" else GATE_Z) + chunk
+            return both[:, row : row + 1]
+
+        bias = {}
+
+        def spread_bias(kind, chunk):
+            spread = banks.tile([P, N_TILE], F32, tag="bank", name="spread")
+            nc.tensor.matmul(
+                out=spread[:],
+                lhsT=selector(kind, chunk).to_broadcast([P, P]),
+                rhs=bias_rows[:],
+                start=True,
+                stop=True,
+            )
+            table = keep.tile([P, N_TILE], F32, name="bias_%s_%d" % (kind, chunk))
+            nc.scalar.copy(out=table[:], in_=spread[:])
+            bias[(kind, chunk)] = table
+
+        tables = [(kind, chunk) for kind in ("i_n", "h_n", "r", "z") for chunk in range(CHUNKS)]
+
+        def features(sb, g):
+            return [sb[:, bt, K_PASS * g : K_PASS * (g + 1)] for bt in range(BATCH_TILES)]
+
+        sources = [features(x_sb, 0), features(z_sb, 0), features(a_sb, 0)]
+        sources += [features(h_sb, g) for g in range(PASSES)]
+        grouped, codes, code_scales = [], [], []
+
+        def transpose_source(s):
+            flipped = banks.tile([P, 2, BATCH_TILES * P], F32, tag="bank", name="flipped")
+            for bt in range(BATCH_TILES):
+                pairs = sources[s][bt].bitcast(F32)
+                for v in range(2):
+                    nc.tensor.transpose(
+                        flipped[:, v, P * bt : P * (bt + 1)], pairs[:, v : K_PASS // 2 : 2], ident_f32[:]
+                    )
+            together = stage.tile([P, 4 * BATCH_TILES * P], BF16, name="together", align_bytes=64)
+            nc.vector.tensor_copy(
+                out=together[:].bitcast(F32).rearrange("p (b v) -> p b v", v=2),
+                in_=flipped[:].rearrange("p v b -> p b v"),
+            )
+            grouped.append(together)
+
+        def quantise_source(s):
+            words = keep.tile([P, BATCH_TILES * P], U32, name="codes_%d" % s, align_bytes=64)
+            scales = keep.tile([P, BATCH_TILES * P], U8, name="code_scales_%d" % s, align_bytes=64)
+            nc.vector.quantize_mx(out=words[:].bitcast(FP8X4), scales=scales[:], in_=grouped[s][:])
+            codes.append(words)
+            code_scales.append(scales)
+
+        for s in range(len(sources)):
+            spread_bias(*tables[2 * s])
+            spread_bias(*tables[2 * s + 1])
+            transpose_source(s)
+            if s > 0:
+                quantise_source(s - 1)
+        quantise_source(len(sources) - 1)
+
+        def operands(first_source, words, plane):
+            return [(first_source + g, words[g], plane[:, g, :]) for g in range(PASSES)]
+
+        def mx_sums(passes, chunk):
+            sums = [banks.tile([P, N_TILE], F32, tag="bank", name="sums") for bt in range(BATCH_TILES)]
+            for i, (s, words, plane) in enumerate(passes):
+                for bt in range(BATCH_TILES):
+                    rows = slice(P * bt, P * (bt + 1))
+                    nc.tensor.matmul_mx(
+                        out=sums[bt][:],
+                        lhsT=codes[s][:, rows].bitcast(FP8X4),
+                        lhsT_scale=code_scales[s][:, rows],
+                        rhs=words[:, 2 * N_TILE * chunk : 2 * N_TILE * (chunk + 1)].bitcast(FP4X4),
+                        rhs_scale=plane[:, N_TILE * chunk : N_TILE * (chunk + 1)],
+                        start=(i == 0),
+                        stop=(i == len(passes) - 1),
+                    )
+            return sums
+
+        def gate_passes(gate):
+            return operands(0, ih_words[gate], ih_plane[gate]) + operands(PASSES, hh_words[gate], hh_plane[gate])
+
+        def sigmoid_gate(kind, sums, chunk):
+            gates = []
+            for bt in range(BATCH_TILES):
+                pre = work.tile([P, N_TILE], F32, name="pre")
+                nc.vector.tensor_tensor(out=pre[:], in0=sums[bt][:], in1=bias[(kind, chunk)][:], op=ALU.add)
+                gate = work.tile([P, N_TILE], F32, name="gate")
+                nc.scalar.activation(out=gate[:], in_=pre[:], func=ACT.Sigmoid)
+                gates.append(gate)
+            return gates
+
+        first, second = {}, {}
+        pieces = [(chunk, bt) for chunk in range(CHUNKS) for bt in range(BATCH_TILES)]
+        for chunk, bt in pieces:
+            first[(chunk, bt)] = keep.tile([P, N_TILE], F32, name="first_%d_%d" % (chunk, bt))
+            second[(chunk, bt)] = keep.tile([P, N_TILE], F32, name="second_%d_%d" % (chunk, bt))
+
+        for kind, passes, target in (
+            ("i_n", operands(0, ih_words[GATE_N], ih_plane[GATE_N]), first),
+            ("h_n", operands(PASSES, hh_words[GATE_N], hh_plane[GATE_N]), second),
+        ):
+            for chunk in range(CHUNKS):
+                sums = mx_sums(passes, chunk)
+                for bt in range(BATCH_TILES):
+                    nc.vector.tensor_tensor(
+                        out=target[(chunk, bt)][:], in0=sums[bt][:], in1=bias[(kind, chunk)][:], op=ALU.add
+                    )
+
+        for chunk in range(CHUNKS):
+            r = sigmoid_gate("r", mx_sums(gate_passes(GATE_R), chunk), chunk)
+            for bt in range(BATCH_TILES):
+                t = second[(chunk, bt)]
+                nc.vector.tensor_tensor(out=t[:], in0=t[:], in1=r[bt][:], op=ALU.mult)
+            for bt in range(BATCH_TILES):
+                n = first[(chunk, bt)]
+                nc.vector.tensor_tensor(out=n[:], in0=n[:], in1=second[(chunk, bt)][:], op=ALU.add)
+            for bt in range(BATCH_TILES):
+                n = first[(chunk, bt)]
+                nc.scalar.activation(out=n[:], in_=n[:], func=ACT.Tanh)
+            for bt in range(BATCH_TILES):
+                nc.gpsimd.tensor_tensor(
+                    out=second[(chunk, bt)][:],
+                    in0=h_sb[:, bt, N_TILE * chunk : N_TILE * (chunk + 1)],
+                    in1=first[(chunk, bt)][:],
+                    op=ALU.subtract,
+                )
+
+        for chunk in range(CHUNKS):
+            zg = sigmoid_gate("z", mx_sums(gate_passes(GATE_Z), chunk), chunk)
+            for bt in range(BATCH_TILES):
+                d = second[(chunk, bt)]
+                nc.vector.tensor_tensor(out=d[:], in0=d[:], in1=zg[bt][:], op=ALU.mult)
+            for bt in range(BATCH_TILES):
+                h_t = first[(chunk, bt)]
+                nc.vector.tensor_tensor(out=h_t[:], in0=h_t[:], in1=second[(chunk, bt)][:], op=ALU.add)
+            for bt in range(BATCH_TILES):
+                nc.sync.dma_start(
+                    out=out[P * bt : P * (bt + 1), N_TILE * chunk : N_TILE * (chunk + 1)],
+                    in_=first[(chunk, bt)][:],
+                )

@@ -38,7 +38,7 @@ def tile_vrnncell_pc_kernel(
         ctx.enter_context(tc.manual_schedule())
 
         bias_rows = keep.tile([P, N_TILE], BF16, name="bias_rows")
-        nc.vector.memset(bias_rows[:].bitcast(I32), 0)
+        nc.gpsimd.memset(bias_rows[:], 0.0)
         nc.scalar.dma_start(out=bias_rows[0:BIAS_ROWS, :], in_=b_ih.rearrange("(s n) -> s n", n=N_TILE))
         nc.scalar.dma_start(
             out=bias_rows[BIAS_ROWS : 2 * BIAS_ROWS, :], in_=b_hh.rearrange("(s n) -> s n", n=N_TILE)
@@ -51,15 +51,13 @@ def tile_vrnncell_pc_kernel(
         ident_f32 = keep.tile([P, P], F32, name="ident_f32")
         make_identity(nc, ident_f32[:])
 
-        def load_activation(dram, features, name):
-            sb = keep.tile([P, BATCH_TILES, features], BF16, name=name)
-            nc.sync.dma_start(out=sb[:], in_=dram.rearrange("(t p) k -> p t k", p=P))
+        def load_features(dram, first_column, name):
+            sb = keep.tile([P, BATCH_TILES, K_PASS], BF16, name=name)
+            nc.sync.dma_start(
+                out=sb[:],
+                in_=dram[:, first_column : first_column + K_PASS].rearrange("(t p) k -> p t k", p=P),
+            )
             return sb
-
-        x_sb = load_activation(x_t, K_PASS, "x_sb")
-        z_sb = load_activation(z_t, K_PASS, "z_sb")
-        a_sb = load_activation(a_prev, K_PASS, "a_sb")
-        h_sb = load_activation(h_prev, HIDDEN, "h_sb")
 
         def load_scales(scales, gate, name):
             plane = keep.tile([P, PASSES, HIDDEN], U8, name=name, align_bytes=64)
@@ -73,27 +71,35 @@ def tile_vrnncell_pc_kernel(
                 )
             return plane
 
-        def load_words(words, gate, name):
-            tiles = []
-            for g in range(PASSES):
-                w = keep.tile([P, 2 * HIDDEN], U8, name="%s_%d" % (name, g), align_bytes=64)
-                nc.sync.dma_start(
-                    out=w[:].bitcast(I32),
-                    in_=words[g, :, 2 * HIDDEN * gate : 2 * HIDDEN * (gate + 1)].bitcast(I32),
-                )
-                tiles.append(w)
-            return tiles
+        def load_words(words, gate, chunk, name):
+            w = keep.tile([P, PASSES, 2 * N_TILE], U8, name=name, align_bytes=64)
+            first_byte = 2 * (HIDDEN * gate + N_TILE * chunk)
+            nc.sync.dma_start(
+                out=w[:].bitcast(I32),
+                in_=words[:, :, first_byte : first_byte + 2 * N_TILE].rearrange("g p n -> p g n").bitcast(I32),
+            )
+            return w
 
+        sources = [
+            load_features(x_t, 0, "x_sb"),
+            load_features(z_t, 0, "z_sb"),
+            load_features(a_prev, 0, "a_sb"),
+        ]
         ih_plane, hh_plane, ih_words, hh_words = {}, {}, {}, {}
         ih_plane[GATE_N] = load_scales(w_ih_scales, GATE_N, "ih_plane_n")
-        ih_words[GATE_N] = load_words(w_ih_words, GATE_N, "ih_words_n")
+        for chunk in range(CHUNKS):
+            ih_words[(GATE_N, chunk)] = load_words(w_ih_words, GATE_N, chunk, "ih_words_n%d" % chunk)
+        for g in range(PASSES):
+            sources.append(load_features(h_prev, K_PASS * g, "h_sb%d" % g))
         hh_plane[GATE_N] = load_scales(w_hh_scales, GATE_N, "hh_plane_n")
-        hh_words[GATE_N] = load_words(w_hh_words, GATE_N, "hh_words_n")
+        for chunk in range(CHUNKS):
+            hh_words[(GATE_N, chunk)] = load_words(w_hh_words, GATE_N, chunk, "hh_words_n%d" % chunk)
         for gate, label in ((GATE_R, "r"), (GATE_Z, "z")):
             ih_plane[gate] = load_scales(w_ih_scales, gate, "ih_plane_" + label)
             hh_plane[gate] = load_scales(w_hh_scales, gate, "hh_plane_" + label)
-            ih_words[gate] = load_words(w_ih_words, gate, "ih_words_" + label)
-            hh_words[gate] = load_words(w_hh_words, gate, "hh_words_" + label)
+            for chunk in range(CHUNKS):
+                ih_words[(gate, chunk)] = load_words(w_ih_words, gate, chunk, "ih_words_%s%d" % (label, chunk))
+                hh_words[(gate, chunk)] = load_words(w_hh_words, gate, chunk, "hh_words_%s%d" % (label, chunk))
 
         both = keep.tile([P, 2 * CHUNKS], BF16, name="both")
         nc.vector.tensor_tensor(
@@ -115,32 +121,26 @@ def tile_vrnncell_pc_kernel(
 
         bias = {}
 
-        def spread_bias(kind, chunk):
-            spread = banks.tile([P, N_TILE], F32, tag="bank", name="spread")
-            nc.tensor.matmul(
-                out=spread[:],
-                lhsT=selector(kind, chunk).to_broadcast([P, P]),
-                rhs=bias_rows[:],
-                start=True,
-                stop=True,
-            )
-            table = keep.tile([P, N_TILE], F32, name="bias_%s_%d" % (kind, chunk))
-            nc.scalar.copy(out=table[:], in_=spread[:])
-            bias[(kind, chunk)] = table
+        def spread_bias(kind):
+            for chunk in range(CHUNKS):
+                spread = banks.tile([P, N_TILE], F32, tag="bank", name="spread")
+                nc.tensor.matmul(
+                    out=spread[:],
+                    lhsT=selector(kind, chunk).to_broadcast([P, P]),
+                    rhs=bias_rows[:],
+                    start=True,
+                    stop=True,
+                )
+                table = keep.tile([P, N_TILE], F32, name="bias_%s_%d" % (kind, chunk))
+                nc.scalar.copy(out=table[:], in_=spread[:])
+                bias[(kind, chunk)] = table
 
-        tables = [(kind, chunk) for kind in ("i_n", "h_n", "r", "z") for chunk in range(CHUNKS)]
-
-        def features(sb, g):
-            return [sb[:, bt, K_PASS * g : K_PASS * (g + 1)] for bt in range(BATCH_TILES)]
-
-        sources = [features(x_sb, 0), features(z_sb, 0), features(a_sb, 0)]
-        sources += [features(h_sb, g) for g in range(PASSES)]
-        grouped, codes, code_scales = [], [], []
+        grouped, codes, code_scales = {}, {}, {}
 
         def transpose_source(s):
             flipped = banks.tile([P, 2, BATCH_TILES * P], F32, tag="bank", name="flipped")
             for bt in range(BATCH_TILES):
-                pairs = sources[s][bt].bitcast(F32)
+                pairs = sources[s][:, bt, :].bitcast(F32)
                 for v in range(2):
                     nc.tensor.transpose(
                         flipped[:, v, P * bt : P * (bt + 1)], pairs[:, v : K_PASS // 2 : 2], ident_f32[:]
@@ -150,54 +150,46 @@ def tile_vrnncell_pc_kernel(
                 out=together[:].bitcast(F32).rearrange("p (b v) -> p b v", v=2),
                 in_=flipped[:].rearrange("p v b -> p b v"),
             )
-            grouped.append(together)
+            grouped[s] = together
 
         def quantise_source(s):
             words = keep.tile([P, BATCH_TILES * P], U32, name="codes_%d" % s, align_bytes=64)
             scales = keep.tile([P, BATCH_TILES * P], U8, name="code_scales_%d" % s, align_bytes=64)
             nc.vector.quantize_mx(out=words[:].bitcast(FP8X4), scales=scales[:], in_=grouped[s][:])
-            codes.append(words)
-            code_scales.append(scales)
+            codes[s] = words
+            code_scales[s] = scales
 
-        for s in range(len(sources)):
-            spread_bias(*tables[2 * s])
-            spread_bias(*tables[2 * s + 1])
-            transpose_source(s)
-            if s > 0:
-                quantise_source(s - 1)
-        quantise_source(len(sources) - 1)
+        def prepare_three(first_source, kinds):
+            transpose_source(first_source)
+            transpose_source(first_source + 1)
+            quantise_source(first_source)
+            transpose_source(first_source + 2)
+            quantise_source(first_source + 1)
+            for kind in kinds:
+                spread_bias(kind)
+            quantise_source(first_source + 2)
 
-        def operands(first_source, words, plane):
-            return [(first_source + g, words[g], plane[:, g, :]) for g in range(PASSES)]
-
-        def mx_sums(passes, chunk):
-            sums = [banks.tile([P, N_TILE], F32, tag="bank", name="sums") for bt in range(BATCH_TILES)]
-            for i, (s, words, plane) in enumerate(passes):
-                for bt in range(BATCH_TILES):
-                    rows = slice(P * bt, P * (bt + 1))
-                    nc.tensor.matmul_mx(
-                        out=sums[bt][:],
-                        lhsT=codes[s][:, rows].bitcast(FP8X4),
-                        lhsT_scale=code_scales[s][:, rows],
-                        rhs=words[:, 2 * N_TILE * chunk : 2 * N_TILE * (chunk + 1)].bitcast(FP4X4),
-                        rhs_scale=plane[:, N_TILE * chunk : N_TILE * (chunk + 1)],
-                        start=(i == 0),
-                        stop=(i == len(passes) - 1),
-                    )
+        def mx_sums(operands, chunk, bt):
+            sums = banks.tile([P, N_TILE], F32, tag="bank", name="sums")
+            rows = slice(P * bt, P * (bt + 1))
+            passes = [(first + g, words, plane, g) for first, words, plane in operands for g in range(PASSES)]
+            for i, (s, words, plane, g) in enumerate(passes):
+                nc.tensor.matmul_mx(
+                    out=sums[:],
+                    lhsT=codes[s][:, rows].bitcast(FP8X4),
+                    lhsT_scale=code_scales[s][:, rows],
+                    rhs=words[:, g, :].bitcast(FP4X4),
+                    rhs_scale=plane[:, g, N_TILE * chunk : N_TILE * (chunk + 1)],
+                    start=(i == 0),
+                    stop=(i == len(passes) - 1),
+                )
             return sums
 
-        def gate_passes(gate):
-            return operands(0, ih_words[gate], ih_plane[gate]) + operands(PASSES, hh_words[gate], hh_plane[gate])
+        def input_side(gate, chunk):
+            return (0, ih_words[(gate, chunk)], ih_plane[gate])
 
-        def sigmoid_gate(kind, sums, chunk):
-            gates = []
-            for bt in range(BATCH_TILES):
-                pre = work.tile([P, N_TILE], F32, name="pre")
-                nc.vector.tensor_tensor(out=pre[:], in0=sums[bt][:], in1=bias[(kind, chunk)][:], op=ALU.add)
-                gate = work.tile([P, N_TILE], F32, name="gate")
-                nc.scalar.activation(out=gate[:], in_=pre[:], func=ACT.Sigmoid)
-                gates.append(gate)
-            return gates
+        def hidden_side(gate, chunk):
+            return (PASSES, hh_words[(gate, chunk)], hh_plane[gate])
 
         first, second = {}, {}
         pieces = [(chunk, bt) for chunk in range(CHUNKS) for bt in range(BATCH_TILES)]
@@ -205,46 +197,59 @@ def tile_vrnncell_pc_kernel(
             first[(chunk, bt)] = keep.tile([P, N_TILE], F32, name="first_%d_%d" % (chunk, bt))
             second[(chunk, bt)] = keep.tile([P, N_TILE], F32, name="second_%d_%d" % (chunk, bt))
 
-        for kind, passes, target in (
-            ("i_n", operands(0, ih_words[GATE_N], ih_plane[GATE_N]), first),
-            ("h_n", operands(PASSES, hh_words[GATE_N], hh_plane[GATE_N]), second),
-        ):
-            for chunk in range(CHUNKS):
-                sums = mx_sums(passes, chunk)
-                for bt in range(BATCH_TILES):
-                    nc.vector.tensor_tensor(
-                        out=target[(chunk, bt)][:], in0=sums[bt][:], in1=bias[(kind, chunk)][:], op=ALU.add
-                    )
+        def add_bias(target, sums, kind, chunk):
+            nc.vector.tensor_tensor(out=target[:], in0=sums[:], in1=bias[(kind, chunk)][:], op=ALU.add)
 
-        for chunk in range(CHUNKS):
-            r = sigmoid_gate("r", mx_sums(gate_passes(GATE_R), chunk), chunk)
-            for bt in range(BATCH_TILES):
-                t = second[(chunk, bt)]
-                nc.vector.tensor_tensor(out=t[:], in0=t[:], in1=r[bt][:], op=ALU.mult)
-            for bt in range(BATCH_TILES):
-                n = first[(chunk, bt)]
-                nc.vector.tensor_tensor(out=n[:], in0=n[:], in1=second[(chunk, bt)][:], op=ALU.add)
-            for bt in range(BATCH_TILES):
-                n = first[(chunk, bt)]
-                nc.scalar.activation(out=n[:], in_=n[:], func=ACT.Tanh)
-            for bt in range(BATCH_TILES):
-                nc.gpsimd.tensor_tensor(
-                    out=second[(chunk, bt)][:],
-                    in0=h_sb[:, bt, N_TILE * chunk : N_TILE * (chunk + 1)],
-                    in1=first[(chunk, bt)][:],
-                    op=ALU.subtract,
-                )
+        def sigmoid_gate(sums, kind, chunk):
+            pre = work.tile([P, N_TILE], F32, name="pre")
+            add_bias(pre, sums, kind, chunk)
+            gate = work.tile([P, N_TILE], F32, name="gate")
+            nc.scalar.activation(out=gate[:], in_=pre[:], func=ACT.Sigmoid)
+            return gate
 
-        for chunk in range(CHUNKS):
-            zg = sigmoid_gate("z", mx_sums(gate_passes(GATE_Z), chunk), chunk)
-            for bt in range(BATCH_TILES):
-                d = second[(chunk, bt)]
-                nc.vector.tensor_tensor(out=d[:], in0=d[:], in1=zg[bt][:], op=ALU.mult)
-            for bt in range(BATCH_TILES):
-                h_t = first[(chunk, bt)]
-                nc.vector.tensor_tensor(out=h_t[:], in0=h_t[:], in1=second[(chunk, bt)][:], op=ALU.add)
-            for bt in range(BATCH_TILES):
-                nc.sync.dma_start(
-                    out=out[P * bt : P * (bt + 1), N_TILE * chunk : N_TILE * (chunk + 1)],
-                    in_=first[(chunk, bt)][:],
-                )
+        def times_gate(piece, gate):
+            nc.vector.tensor_tensor(out=second[piece][:], in0=second[piece][:], in1=gate[:], op=ALU.mult)
+
+        def add_second(piece):
+            nc.vector.tensor_tensor(out=first[piece][:], in0=first[piece][:], in1=second[piece][:], op=ALU.add)
+
+        def candidate(piece):
+            chunk, bt = piece
+            add_second(piece)
+            nc.scalar.activation(out=first[piece][:], in_=first[piece][:], func=ACT.Tanh)
+            nc.gpsimd.tensor_tensor(
+                out=second[piece][:], in0=sources[PASSES + chunk][:, bt, :], in1=first[piece][:], op=ALU.subtract
+            )
+
+        def finish(piece):
+            chunk, bt = piece
+            add_second(piece)
+            nc.sync.dma_start(
+                out=out[P * bt : P * (bt + 1), N_TILE * chunk : N_TILE * (chunk + 1)], in_=first[piece][:]
+            )
+
+        spread_bias("i_n")
+        prepare_three(0, ["h_n"])
+        for chunk, bt in pieces:
+            add_bias(first[(chunk, bt)], mx_sums([input_side(GATE_N, chunk)], chunk, bt), "i_n", chunk)
+        prepare_three(PASSES, ["r", "z"])
+        for chunk, bt in pieces:
+            add_bias(second[(chunk, bt)], mx_sums([hidden_side(GATE_N, chunk)], chunk, bt), "h_n", chunk)
+
+        gates = {}
+        steps = [(GATE_R, "r", piece) for piece in pieces] + [(GATE_Z, "z", piece) for piece in pieces]
+        before = None
+        for gate, kind, piece in steps:
+            chunk, bt = piece
+            sums = mx_sums([input_side(gate, chunk), hidden_side(gate, chunk)], chunk, bt)
+            if before is not None:
+                times_gate(before[1], gates[before])
+            gates[(kind, piece)] = sigmoid_gate(sums, kind, chunk)
+            if before is not None:
+                if before[0] == "r":
+                    candidate(before[1])
+                else:
+                    finish(before[1])
+            before = (kind, piece)
+        times_gate(before[1], gates[before])
+        finish(before[1])

@@ -137,7 +137,7 @@ def tile_vrnncell_pc_kernel(
 
         grouped, codes, code_scales = {}, {}, {}
 
-        def transpose_source(s):
+        def transpose_source(s, copier):
             flipped = banks.tile([P, 2, BATCH_TILES * P], F32, tag="bank", name="flipped")
             for bt in range(BATCH_TILES):
                 pairs = sources[s][:, bt, :].bitcast(F32)
@@ -146,7 +146,7 @@ def tile_vrnncell_pc_kernel(
                         flipped[:, v, P * bt : P * (bt + 1)], pairs[:, v : K_PASS // 2 : 2], ident_f32[:]
                     )
             together = stage.tile([P, 4 * BATCH_TILES * P], BF16, name="together", align_bytes=64)
-            nc.vector.tensor_copy(
+            copier(
                 out=together[:].bitcast(F32).rearrange("p (b v) -> p b v", v=2),
                 in_=flipped[:].rearrange("p v b -> p b v"),
             )
@@ -159,11 +159,11 @@ def tile_vrnncell_pc_kernel(
             codes[s] = words
             code_scales[s] = scales
 
-        def prepare_three(first_source, kinds):
-            transpose_source(first_source)
-            transpose_source(first_source + 1)
+        def prepare_three(first_source, kinds, copier):
+            transpose_source(first_source, copier)
+            transpose_source(first_source + 1, copier)
             quantise_source(first_source)
-            transpose_source(first_source + 2)
+            transpose_source(first_source + 2, copier)
             quantise_source(first_source + 1)
             for kind in kinds:
                 spread_bias(kind)
@@ -229,27 +229,31 @@ def tile_vrnncell_pc_kernel(
             )
 
         spread_bias("i_n")
-        prepare_three(0, ["h_n"])
+        prepare_three(0, ["h_n"], nc.vector.tensor_copy)
         for chunk, bt in pieces:
             add_bias(first[(chunk, bt)], mx_sums([input_side(GATE_N, chunk)], chunk, bt), "i_n", chunk)
-        prepare_three(PASSES, ["r", "z"])
+        prepare_three(PASSES, ["r", "z"], nc.scalar.copy)
         for chunk, bt in pieces:
             add_bias(second[(chunk, bt)], mx_sums([hidden_side(GATE_N, chunk)], chunk, bt), "h_n", chunk)
 
         gates = {}
         steps = [(GATE_R, "r", piece) for piece in pieces] + [(GATE_Z, "z", piece) for piece in pieces]
-        before = None
-        for gate, kind, piece in steps:
+
+        def close(step):
+            if step[1] == "r":
+                candidate(step[2])
+            else:
+                finish(step[2])
+
+        for i, (gate, kind, piece) in enumerate(steps):
             chunk, bt = piece
             sums = mx_sums([input_side(gate, chunk), hidden_side(gate, chunk)], chunk, bt)
-            if before is not None:
-                times_gate(before[1], gates[before])
-            gates[(kind, piece)] = sigmoid_gate(sums, kind, chunk)
-            if before is not None:
-                if before[0] == "r":
-                    candidate(before[1])
-                else:
-                    finish(before[1])
-            before = (kind, piece)
-        times_gate(before[1], gates[before])
-        finish(before[1])
+            gates[i] = sigmoid_gate(sums, kind, chunk)
+            if i >= 1:
+                times_gate(steps[i - 1][2], gates[i - 1])
+            if i >= 2:
+                close(steps[i - 2])
+        last = len(steps) - 1
+        times_gate(steps[last][2], gates[last])
+        close(steps[last - 1])
+        close(steps[last])

@@ -22,6 +22,7 @@ N_TILE = 512
 CHUNKS = HIDDEN // N_TILE
 GATE_R, GATE_Z, GATE_N = 0, 1, 2
 BIAS_ROWS = 3 * CHUNKS
+WARM_UP_MATMULS = 8
 
 FLOPS = 2 * 2 * 256 * 1536 * 4608
 
@@ -43,6 +44,11 @@ def tile_vrnncell_pc_kernel(
         nc.scalar.dma_start(
             out=bias_rows[BIAS_ROWS : 2 * BIAS_ROWS, :], in_=b_hh.rearrange("(s n) -> s n", n=N_TILE)
         )
+        zeros = keep.tile([P, N_TILE], BF16, name="zeros")
+        nc.vector.memset(zeros[:], 0.0)
+        unread = banks.tile([P, N_TILE], F32, tag="bank", name="unread")
+        for i in range(WARM_UP_MATMULS):
+            nc.tensor.matmul(out=unread[:], lhsT=zeros[:, 0:P], rhs=zeros[:], start=True, stop=True)
         warm = keep.tile([P, 1], F32, name="warm")
         nc.vector.memset(warm[:], 0.0)
         nc.scalar.activation(out=warm[:], in_=warm[:], func=ACT.Sigmoid)
@@ -59,17 +65,18 @@ def tile_vrnncell_pc_kernel(
             )
             return sb
 
-        def load_scales(scales, gate, name):
+        def zeroed_plane(name, memset, view, zero):
             plane = keep.tile([P, PASSES, HIDDEN], U8, name=name, align_bytes=64)
-            nc.vector.memset(plane[:].bitcast(I32), 0)
-            columns = scales[:, :, HIDDEN * gate : HIDDEN * (gate + 1)]
-            for q in range(8):
-                partition = 32 * (q // 4) + q % 4
-                nc.sync.dma_start(
-                    out=plane[partition:P:64, :, :].bitcast(I32),
-                    in_=columns[:, q:16:8, :].rearrange("g j n -> j g n").bitcast(I32),
-                )
+            memset(plane[:].bitcast(view), zero)
             return plane
+
+        def load_scales(plane, scales, gate):
+            columns = scales[:, :, HIDDEN * gate : HIDDEN * (gate + 1)]
+            for j in range(4):
+                nc.sync.dma_start(
+                    out=plane[j:P:32, :, :].bitcast(I32),
+                    in_=columns[:, j:16:4, :].rearrange("g q n -> q g n").bitcast(I32),
+                )
 
         def load_words(words, gate, chunk, name):
             w = keep.tile([P, PASSES, 2 * N_TILE], U8, name=name, align_bytes=64)
@@ -86,20 +93,31 @@ def tile_vrnncell_pc_kernel(
             load_features(a_prev, 0, "a_sb"),
         ]
         ih_plane, hh_plane, ih_words, hh_words = {}, {}, {}, {}
-        ih_plane[GATE_N] = load_scales(w_ih_scales, GATE_N, "ih_plane_n")
+        ih_plane[GATE_N] = zeroed_plane("ih_plane_n", nc.vector.memset, I32, 0)
+        load_scales(ih_plane[GATE_N], w_ih_scales, GATE_N)
         for chunk in range(CHUNKS):
             ih_words[(GATE_N, chunk)] = load_words(w_ih_words, GATE_N, chunk, "ih_words_n%d" % chunk)
         for g in range(PASSES):
             sources.append(load_features(h_prev, K_PASS * g, "h_sb%d" % g))
-        hh_plane[GATE_N] = load_scales(w_hh_scales, GATE_N, "hh_plane_n")
+        hh_plane[GATE_N] = zeroed_plane("hh_plane_n", nc.vector.memset, I32, 0)
+        load_scales(hh_plane[GATE_N], w_hh_scales, GATE_N)
         for chunk in range(CHUNKS):
             hh_words[(GATE_N, chunk)] = load_words(w_hh_words, GATE_N, chunk, "hh_words_n%d" % chunk)
-        for gate, label in ((GATE_R, "r"), (GATE_Z, "z")):
-            ih_plane[gate] = load_scales(w_ih_scales, gate, "ih_plane_" + label)
-            hh_plane[gate] = load_scales(w_hh_scales, gate, "hh_plane_" + label)
-            for chunk in range(CHUNKS):
-                ih_words[(gate, chunk)] = load_words(w_ih_words, gate, chunk, "ih_words_%s%d" % (label, chunk))
-                hh_words[(gate, chunk)] = load_words(w_hh_words, gate, chunk, "hh_words_%s%d" % (label, chunk))
+        ih_plane[GATE_R] = zeroed_plane("ih_plane_r", nc.vector.memset, I32, 0)
+        load_scales(ih_plane[GATE_R], w_ih_scales, GATE_R)
+        ih_plane[GATE_Z] = zeroed_plane("ih_plane_z", nc.gpsimd.memset, F32, 0.0)
+        hh_plane[GATE_Z] = zeroed_plane("hh_plane_z", nc.gpsimd.memset, F32, 0.0)
+
+        def load_rest():
+            hh_plane[GATE_R] = zeroed_plane("hh_plane_r", nc.vector.memset, I32, 0)
+            load_scales(hh_plane[GATE_R], w_hh_scales, GATE_R)
+            for gate, label in ((GATE_R, "r"), (GATE_Z, "z")):
+                if gate == GATE_Z:
+                    load_scales(ih_plane[GATE_Z], w_ih_scales, GATE_Z)
+                    load_scales(hh_plane[GATE_Z], w_hh_scales, GATE_Z)
+                for chunk in range(CHUNKS):
+                    ih_words[(gate, chunk)] = load_words(w_ih_words, gate, chunk, "ih_words_%s%d" % (label, chunk))
+                    hh_words[(gate, chunk)] = load_words(w_hh_words, gate, chunk, "hh_words_%s%d" % (label, chunk))
 
         both = keep.tile([P, 2 * CHUNKS], BF16, name="both")
         nc.vector.tensor_tensor(
@@ -121,19 +139,18 @@ def tile_vrnncell_pc_kernel(
 
         bias = {}
 
-        def spread_bias(kind):
-            for chunk in range(CHUNKS):
-                spread = banks.tile([P, N_TILE], F32, tag="bank", name="spread")
-                nc.tensor.matmul(
-                    out=spread[:],
-                    lhsT=selector(kind, chunk).to_broadcast([P, P]),
-                    rhs=bias_rows[:],
-                    start=True,
-                    stop=True,
-                )
-                table = keep.tile([P, N_TILE], F32, name="bias_%s_%d" % (kind, chunk))
-                nc.scalar.copy(out=table[:], in_=spread[:])
-                bias[(kind, chunk)] = table
+        def spread_bias(kind, chunk):
+            spread = banks.tile([P, N_TILE], F32, tag="bank", name="spread")
+            nc.tensor.matmul(
+                out=spread[:],
+                lhsT=selector(kind, chunk).to_broadcast([P, P]),
+                rhs=bias_rows[:],
+                start=True,
+                stop=True,
+            )
+            table = keep.tile([P, N_TILE], F32, name="bias_%s_%d" % (kind, chunk))
+            nc.scalar.copy(out=table[:], in_=spread[:])
+            bias[(kind, chunk)] = table
 
         grouped, codes, code_scales = {}, {}, {}
 
@@ -159,14 +176,15 @@ def tile_vrnncell_pc_kernel(
             codes[s] = words
             code_scales[s] = scales
 
-        def prepare_three(first_source, kinds, copier):
-            transpose_source(first_source, copier)
-            transpose_source(first_source + 1, copier)
+        def prepare_three(first_source, kinds, copiers):
+            transpose_source(first_source, copiers[0])
+            transpose_source(first_source + 1, copiers[1])
             quantise_source(first_source)
-            transpose_source(first_source + 2, copier)
+            transpose_source(first_source + 2, copiers[2])
             quantise_source(first_source + 1)
             for kind in kinds:
-                spread_bias(kind)
+                for chunk in range(CHUNKS):
+                    spread_bias(kind, chunk)
             quantise_source(first_source + 2)
 
         def mx_sums(operands, chunk, bt):
@@ -228,11 +246,12 @@ def tile_vrnncell_pc_kernel(
                 out=out[P * bt : P * (bt + 1), N_TILE * chunk : N_TILE * (chunk + 1)], in_=first[piece][:]
             )
 
-        spread_bias("i_n")
-        prepare_three(0, ["h_n"], nc.vector.tensor_copy)
+        prepare_three(0, ["i_n"], [nc.scalar.copy, nc.vector.tensor_copy, nc.scalar.copy])
         for chunk, bt in pieces:
             add_bias(first[(chunk, bt)], mx_sums([input_side(GATE_N, chunk)], chunk, bt), "i_n", chunk)
-        prepare_three(PASSES, ["r", "z"], nc.scalar.copy)
+            if (chunk, bt) == pieces[0]:
+                load_rest()
+        prepare_three(PASSES, ["h_n", "r"], [nc.scalar.copy, nc.scalar.copy, nc.scalar.copy])
         for chunk, bt in pieces:
             add_bias(second[(chunk, bt)], mx_sums([hidden_side(GATE_N, chunk)], chunk, bt), "h_n", chunk)
 
@@ -248,6 +267,8 @@ def tile_vrnncell_pc_kernel(
         for i, (gate, kind, piece) in enumerate(steps):
             chunk, bt = piece
             sums = mx_sums([input_side(gate, chunk), hidden_side(gate, chunk)], chunk, bt)
+            if kind == "r" and bt == 0:
+                spread_bias("z", chunk)
             gates[i] = sigmoid_gate(sums, kind, chunk)
             if i >= 1:
                 times_gate(steps[i - 1][2], gates[i - 1])

@@ -232,10 +232,12 @@ def tile_vrnncell_pc_kernel(
             nc.vector.tensor_tensor(out=first[piece][:], in0=first[piece][:], in1=second[piece][:], op=ALU.add)
 
         def candidate(piece):
-            chunk, bt = piece
             add_second(piece)
             nc.scalar.activation(out=first[piece][:], in_=first[piece][:], func=ACT.Tanh)
-            nc.gpsimd.tensor_tensor(
+
+        def difference(piece):
+            chunk, bt = piece
+            nc.vector.tensor_tensor(
                 out=second[piece][:], in0=sources[PASSES + chunk][:, bt, :], in1=first[piece][:], op=ALU.subtract
             )
 
@@ -274,6 +276,8 @@ def tile_vrnncell_pc_kernel(
                 times_gate(steps[i - 1][2], gates[i - 1])
             if i >= 2:
                 close(steps[i - 2])
+            if i >= 3 and steps[i - 3][1] == "r":
+                difference(steps[i - 3][2])
         last = len(steps) - 1
         times_gate(steps[last][2], gates[last])
         close(steps[last - 1])

from contextlib import ExitStack

import concourse.mybir as mybir
from concourse.masks import make_identity

F32 = mybir.dt.float32
BF16 = mybir.dt.bfloat16
I32 = mybir.dt.int32
U32 = mybir.dt.uint32
U8 = mybir.dt.uint8
FP8X4 = mybir.dt.float8_e4m3fn_x4
FP4X4 = mybir.dt.float4_e2m1fn_x4
ALU = mybir.AluOpType
ACT = mybir.ActivationFunctionType

P = 128
BATCH_TILES = 2
HIDDEN = 1536
K_PASS = 512
PASSES = 3
N_TILE = 512
CHUNKS = HIDDEN // N_TILE
GATE_R, GATE_Z, GATE_N = 0, 1, 2
BIAS_ROWS = 3 * CHUNKS
WARM_UP_MATMULS = 8

FLOPS = 2 * 2 * 256 * 1536 * 4608


def tile_vrnncell_pc_kernel(
    tc, x_t, z_t, a_prev, h_prev, w_ih_words, w_ih_scales, w_hh_words, w_hh_scales, b_ih, b_hh, out
):
    nc = tc.nc
    with ExitStack() as ctx:
        keep = ctx.enter_context(tc.tile_pool(name="keep", bufs=1))
        stage = ctx.enter_context(tc.tile_pool(name="stage", bufs=3))
        work = ctx.enter_context(tc.tile_pool(name="work", bufs=4))
        banks = ctx.enter_context(tc.psum_pool(name="banks", bufs=8))
        ctx.enter_context(tc.manual_schedule())

        bias_rows = keep.tile([P, N_TILE], BF16, name="bias_rows")
        nc.gpsimd.memset(bias_rows[:], 0.0)
        nc.scalar.dma_start(out=bias_rows[0:BIAS_ROWS, :], in_=b_ih.rearrange("(s n) -> s n", n=N_TILE))
        nc.scalar.dma_start(
            out=bias_rows[BIAS_ROWS : 2 * BIAS_ROWS, :], in_=b_hh.rearrange("(s n) -> s n", n=N_TILE)
        )
        zeros = keep.tile([P, N_TILE], BF16, name="zeros")
        nc.vector.memset(zeros[:], 0.0)
        unread = banks.tile([P, N_TILE], F32, tag="bank", name="unread")
        for i in range(WARM_UP_MATMULS):
            nc.tensor.matmul(out=unread[:], lhsT=zeros[:, 0:P], rhs=zeros[:], start=True, stop=True)
        warm = keep.tile([P, 1], F32, name="warm")
        nc.vector.memset(warm[:], 0.0)
        nc.scalar.activation(out=warm[:], in_=warm[:], func=ACT.Sigmoid)
        ident_bf16 = keep.tile([P, P], BF16, name="ident_bf16")
        make_identity(nc, ident_bf16[:])
        ident_f32 = keep.tile([P, P], F32, name="ident_f32")
        make_identity(nc, ident_f32[:])

        def load_features(dram, first_column, name):
            sb = keep.tile([P, BATCH_TILES, K_PASS], BF16, name=name)
            nc.sync.dma_start(
                out=sb[:],
                in_=dram[:, first_column : first_column + K_PASS].rearrange("(t p) k -> p t k", p=P),
            )
            return sb

        def zeroed_plane(name, memset, view, zero):
            plane = keep.tile([P, PASSES, HIDDEN], U8, name=name, align_bytes=64)
            memset(plane[:].bitcast(view), zero)
            return plane

        def load_scales(plane, scales, gate):
            columns = scales[:, :, HIDDEN * gate : HIDDEN * (gate + 1)]
            for j in range(4):
                nc.sync.dma_start(
                    out=plane[j:P:32, :, :].bitcast(I32),
                    in_=columns[:, j:16:4, :].rearrange("g q n -> q g n").bitcast(I32),
                )

        def load_words(words, gate, chunk, name):
            w = keep.tile([P, PASSES, 2 * N_TILE], U8, name=name, align_bytes=64)
            first_byte = 2 * (HIDDEN * gate + N_TILE * chunk)
            nc.sync.dma_start(
                out=w[:].bitcast(I32),
                in_=words[:, :, first_byte : first_byte + 2 * N_TILE].rearrange("g p n -> p g n").bitcast(I32),
            )
            return w

        sources = [
            load_features(x_t, 0, "x_sb"),
            load_features(z_t, 0, "z_sb"),
            load_features(a_prev, 0, "a_sb"),
        ]
        ih_plane, hh_plane, ih_words, hh_words = {}, {}, {}, {}
        ih_plane[GATE_N] = zeroed_plane("ih_plane_n", nc.vector.memset, I32, 0)
        load_scales(ih_plane[GATE_N], w_ih_scales, GATE_N)
        for chunk in range(CHUNKS):
            ih_words[(GATE_N, chunk)] = load_words(w_ih_words, GATE_N, chunk, "ih_words_n%d" % chunk)
        for g in range(PASSES):
            sources.append(load_features(h_prev, K_PASS * g, "h_sb%d" % g))
        hh_plane[GATE_N] = zeroed_plane("hh_plane_n", nc.vector.memset, I32, 0)
        load_scales(hh_plane[GATE_N], w_hh_scales, GATE_N)
        for chunk in range(CHUNKS):
            hh_words[(GATE_N, chunk)] = load_words(w_hh_words, GATE_N, chunk, "hh_words_n%d" % chunk)
        ih_plane[GATE_R] = zeroed_plane("ih_plane_r", nc.vector.memset, I32, 0)
        load_scales(ih_plane[GATE_R], w_ih_scales, GATE_R)
        ih_plane[GATE_Z] = zeroed_plane("ih_plane_z", nc.gpsimd.memset, F32, 0.0)
        hh_plane[GATE_Z] = zeroed_plane("hh_plane_z", nc.gpsimd.memset, F32, 0.0)

        def load_rest():
            hh_plane[GATE_R] = zeroed_plane("hh_plane_r", nc.vector.memset, I32, 0)
            load_scales(hh_plane[GATE_R], w_hh_scales, GATE_R)
            for gate, label in ((GATE_R, "r"), (GATE_Z, "z")):
                if gate == GATE_Z:
                    load_scales(ih_plane[GATE_Z], w_ih_scales, GATE_Z)
                    load_scales(hh_plane[GATE_Z], w_hh_scales, GATE_Z)
                for chunk in range(CHUNKS):
                    ih_words[(gate, chunk)] = load_words(w_ih_words, gate, chunk, "ih_words_%s%d" % (label, chunk))
                    hh_words[(gate, chunk)] = load_words(w_hh_words, gate, chunk, "hh_words_%s%d" % (label, chunk))

        both = keep.tile([P, 2 * CHUNKS], BF16, name="both")
        nc.vector.tensor_tensor(
            out=both[:],
            in0=ident_bf16[:, 0 : 2 * CHUNKS],
            in1=ident_bf16[:, BIAS_ROWS : BIAS_ROWS + 2 * CHUNKS],
            op=ALU.add,
        )

        def selector(kind, chunk):
            if kind == "i_n":
                row = CHUNKS * GATE_N + chunk
                return ident_bf16[:, row : row + 1]
            if kind == "h_n":
                row = BIAS_ROWS + CHUNKS * GATE_N + chunk
                return ident_bf16[:, row : row + 1]
            row = CHUNKS * (GATE_R if kind == "r" else GATE_Z) + chunk
            return both[:, row : row + 1]

        bias = {}

        def spread_bias(kind, chunk):
            spread = banks.tile([P, N_TILE], F32, tag="bank", name="spread")
            nc.tensor.matmul(
                out=spread[:],
                lhsT=selector(kind, chunk).to_broadcast([P, P]),
                rhs=bias_rows[:],
                start=True,
                stop=True,
            )
            table = keep.tile([P, N_TILE], F32, name="bias_%s_%d" % (kind, chunk))
            nc.scalar.copy(out=table[:], in_=spread[:])
            bias[(kind, chunk)] = table

        grouped, codes, code_scales = {}, {}, {}

        def transpose_source(s, copier):
            flipped = banks.tile([P, 2, BATCH_TILES * P], F32, tag="bank", name="flipped")
            for bt in range(BATCH_TILES):
                pairs = sources[s][:, bt, :].bitcast(F32)
                for v in range(2):
                    nc.tensor.transpose(
                        flipped[:, v, P * bt : P * (bt + 1)], pairs[:, v : K_PASS // 2 : 2], ident_f32[:]
                    )
            together = stage.tile([P, 4 * BATCH_TILES * P], BF16, name="together", align_bytes=64)
            copier(
                out=together[:].bitcast(F32).rearrange("p (b v) -> p b v", v=2),
                in_=flipped[:].rearrange("p v b -> p b v"),
            )
            grouped[s] = together

        def quantise_source(s):
            words = keep.tile([P, BATCH_TILES * P], U32, name="codes_%d" % s, align_bytes=64)
            scales = keep.tile([P, BATCH_TILES * P], U8, name="code_scales_%d" % s, align_bytes=64)
            nc.vector.quantize_mx(out=words[:].bitcast(FP8X4), scales=scales[:], in_=grouped[s][:])
            codes[s] = words
            code_scales[s] = scales

        def prepare_three(first_source, kinds, copiers):
            transpose_source(first_source, copiers[0])
            transpose_source(first_source + 1, copiers[1])
            quantise_source(first_source)
            transpose_source(first_source + 2, copiers[2])
            quantise_source(first_source + 1)
            for kind in kinds:
                for chunk in range(CHUNKS):
                    spread_bias(kind, chunk)
            quantise_source(first_source + 2)

        def mx_sums(operands, chunk, bt):
            sums = banks.tile([P, N_TILE], F32, tag="bank", name="sums")
            rows = slice(P * bt, P * (bt + 1))
            passes = [(first + g, words, plane, g) for first, words, plane in operands for g in range(PASSES)]
            for i, (s, words, plane, g) in enumerate(passes):
                nc.tensor.matmul_mx(
                    out=sums[:],
                    lhsT=codes[s][:, rows].bitcast(FP8X4),
                    lhsT_scale=code_scales[s][:, rows],
                    rhs=words[:, g, :].bitcast(FP4X4),
                    rhs_scale=plane[:, g, N_TILE * chunk : N_TILE * (chunk + 1)],
                    start=(i == 0),
                    stop=(i == len(passes) - 1),
                )
            return sums

        def input_side(gate, chunk):
            return (0, ih_words[(gate, chunk)], ih_plane[gate])

        def hidden_side(gate, chunk):
            return (PASSES, hh_words[(gate, chunk)], hh_plane[gate])

        first, second = {}, {}
        pieces = [(chunk, bt) for chunk in range(CHUNKS) for bt in range(BATCH_TILES)]
        for chunk, bt in pieces:
            first[(chunk, bt)] = keep.tile([P, N_TILE], F32, name="first_%d_%d" % (chunk, bt))
            second[(chunk, bt)] = keep.tile([P, N_TILE], F32, name="second_%d_%d" % (chunk, bt))

        def add_bias(target, sums, kind, chunk):
            nc.vector.tensor_tensor(out=target[:], in0=sums[:], in1=bias[(kind, chunk)][:], op=ALU.add)

        def sigmoid_gate(sums, kind, chunk):
            pre = work.tile([P, N_TILE], F32, name="pre")
            add_bias(pre, sums, kind, chunk)
            gate = work.tile([P, N_TILE], F32, name="gate")
            nc.scalar.activation(out=gate[:], in_=pre[:], func=ACT.Sigmoid)
            return gate

        def times_gate(piece, gate):
            nc.vector.tensor_tensor(out=second[piece][:], in0=second[piece][:], in1=gate[:], op=ALU.mult)

        def add_second(piece):
            nc.vector.tensor_tensor(out=first[piece][:], in0=first[piece][:], in1=second[piece][:], op=ALU.add)

        def candidate(piece):
            add_second(piece)
            nc.scalar.activation(out=first[piece][:], in_=first[piece][:], func=ACT.Tanh)

        def difference(piece):
            chunk, bt = piece
            nc.vector.tensor_tensor(
                out=second[piece][:], in0=sources[PASSES + chunk][:, bt, :], in1=first[piece][:], op=ALU.subtract
            )

        def finish(piece):
            chunk, bt = piece
            add_second(piece)
            nc.sync.dma_start(
                out=out[P * bt : P * (bt + 1), N_TILE * chunk : N_TILE * (chunk + 1)], in_=first[piece][:]
            )

        prepare_three(0, ["i_n"], [nc.scalar.copy, nc.vector.tensor_copy, nc.scalar.copy])
        for chunk, bt in pieces:
            add_bias(first[(chunk, bt)], mx_sums([input_side(GATE_N, chunk)], chunk, bt), "i_n", chunk)
            if (chunk, bt) == pieces[0]:
                load_rest()
        prepare_three(PASSES, ["h_n", "r"], [nc.scalar.copy, nc.scalar.copy, nc.scalar.copy])
        for chunk, bt in pieces:
            add_bias(second[(chunk, bt)], mx_sums([hidden_side(GATE_N, chunk)], chunk, bt), "h_n", chunk)

        gates = {}
        steps = [(GATE_R, "r", piece) for piece in pieces] + [(GATE_Z, "z", piece) for piece in pieces]

        def close(step):
            if step[1] == "r":
                candidate(step[2])
            else:
                finish(step[2])

        for i, (gate, kind, piece) in enumerate(steps):
            chunk, bt = piece
            sums = mx_sums([input_side(gate, chunk), hidden_side(gate, chunk)], chunk, bt)
            if kind == "r" and bt == 0:
                spread_bias("z", chunk)
            gates[i] = sigmoid_gate(sums, kind, chunk)
            if i >= 1:
                times_gate(steps[i - 1][2], gates[i - 1])
            if i >= 2:
                close(steps[i - 2])
            if i >= 3 and steps[i - 3][1] == "r":
                difference(steps[i - 3][2])
        last = len(steps) - 1
        times_gate(steps[last][2], gates[last])
        close(steps[last - 1])
        close(steps[last])
